import numpy as np
import ml_dtypes


def mxq(x, axis, fmt="e4m3"):
    dtype, down = {"e4m3": (ml_dtypes.float8_e4m3fn, 7), "e5m2": (ml_dtypes.float8_e5m2, 14)}[fmt]
    v = np.moveaxis(np.asarray(x, np.float32).astype(ml_dtypes.bfloat16).astype(np.float64), axis, -1)
    blocks = v.reshape(v.shape[:-1] + (-1, 32))
    amax = np.abs(blocks).max(-1, keepdims=True)
    byte = np.maximum(np.where(amax > 0, np.frexp(amax)[1] - 1 + 127, 0) - down, 1)
    scale = np.exp2(byte - 127.0)
    codes = (blocks / scale).astype(np.float32).astype(dtype).astype(np.float64)
    return np.moveaxis((codes * scale).reshape(v.shape), -1, axis)


WIDE = False


def mx_kscale(k):
    if not WIDE:
        return np.ones(k)
    levels = np.array([10, -10, 5, -5, 0])
    if k % 512:
        return np.exp2(np.random.permutation(np.resize(levels, k // 32))).repeat(32)
    a = np.empty((k // 512, 16))
    for p in range(k // 512):
        a[p, :8] = np.random.permutation(np.resize(levels, 8))
        for g in range(8):
            far = levels[np.abs(levels - a[p, g]) >= 10]
            a[p, g + 8] = far[np.random.randint(len(far))]
    return np.exp2(a.ravel()).repeat(32)


BF16 = ml_dtypes.bfloat16


def bf(x):
    return np.asarray(x, np.float32).astype(BF16)


def f64(x):
    return np.asarray(x).astype(np.float64)


B, N, K, D, L = 4, 1024, 7, 512, 256


def setup_inputs():
    s = mx_kscale(D)
    limit = np.sqrt(6.0 / (D + L))
    lone = np.random.random((B, N, 1)) < 0.125
    a = (0.3 + 0.7 * np.random.random((B, N, K + 1))) * np.where(lone, 0.4 / (K + 1), 1.0)
    return {"targets": bf(np.random.standard_normal((B, N, D)) * s),
            "neighbors": bf(np.random.standard_normal((B, N, K, D)) * s),
            "a": bf(a),
            "kernel": bf(np.random.uniform(-limit, limit, (D, L)) / s[:, None])}


def reference(targets, neighbors, a, kernel):
    neighborhood = np.concatenate([f64(targets)[..., None, :], f64(neighbors)], axis=-2)
    y = (mxq(neighborhood, 3, "e4m3") @ mxq(f64(kernel), 0, "e4m3")).sum(axis=-2)
    factor = f64(a).sum(axis=-1, keepdims=True)
    factor = np.where(factor > 0.5, factor, np.ones_like(factor))
    y = y / factor
    return np.maximum(y, 0.0)

@@ -1,0 +1,196 @@
+from contextlib import ExitStack
+
+import concourse.mybir as mybir
+from concourse.masks import make_identity
+
+F32 = mybir.dt.float32
+BF16 = mybir.dt.bfloat16
+U32 = mybir.dt.uint32
+U8 = mybir.dt.uint8
+FP8X4 = mybir.dt.float8_e4m3fn_x4
+ALU = mybir.AluOpType
+ACT = mybir.ActivationFunctionType
+
+P = 128
+NODES = 4096
+TILES = NODES // P
+NBRS = 7
+MEMBERS = NBRS + 1
+D = 512
+L = 256
+WORDS = D // 2
+
+FLOPS = 2 * NODES * MEMBERS * D * L
+
+RUNS = [1] * 32
+NB_CHUNKS = [(0, 1), (1, 1)] + [(j, 2) for j in range(2, 30, 2)] + [(30, 1), (31, 1)]
+TG_CHUNKS = [(0, 1), (1, 3), (4, 4), (8, 8), (16, 8), (24, 8)]
+ST_CHUNKS = [(j, 4) for j in range(0, 28, 4)] + [(28, 2), (30, 1), (31, 1)]
+NB_BUFS = 6
+VECTOR_BANKS = ((3,), (1, 3))
+
+
+def tile_singlegcnlayer_t_kernel(tc, targets, neighbors, a, kernel, out):
+    nc = tc.nc
+    tg_v = targets.rearrange("b n d -> (b n) d").rearrange("(p j) d -> p j d", j=TILES)
+    nb_v = neighbors.rearrange("b n k d -> (b n) (k d)").rearrange("(p j) f -> p j f", j=TILES)
+    a_v = a.rearrange("b n k -> (b n) k").rearrange("(p j) k -> p (j k)", j=TILES)
+    out_v = out.rearrange("b n l -> (b n) l").rearrange("(p j) l -> p j l", j=TILES)
+    w_v = kernel.rearrange("(q t) c -> q (t c)", t=4)
+
+    with ExitStack() as ctx:
+        const = ctx.enter_context(tc.tile_pool(name="const", bufs=1))
+        nbp = ctx.enter_context(tc.tile_pool(name="nbp", bufs=NB_BUFS))
+        grp = ctx.enter_context(tc.tile_pool(name="grp", bufs=4))
+        qp = ctx.enter_context(tc.tile_pool(name="qp", bufs=4))
+        stp = ctx.enter_context(tc.tile_pool(name="stp", bufs=3))
+        pst = ctx.enter_context(tc.psum_pool(name="pst", bufs=6))
+        psa = ctx.enter_context(tc.psum_pool(name="psa", bufs=2))
+        ctx.enter_context(tc.manual_schedule())
+
+        ident = const.tile([P, P], F32, name="ident")
+        make_identity(nc, ident[:])
+        warm = const.tile([P, 1], F32, name="warm")
+        nc.scalar.activation(out=warm[:], in_=ident[:, 0:1], func=ACT.Relu)
+
+        src = {}
+        state = {"nb": 0, "tg": 0}
+
+        def load_targets():
+            j0, cnt = TG_CHUNKS[state["tg"]]
+            state["tg"] += 1
+            t = const.tile([P, cnt * D], BF16, name="tg%d" % j0)
+            nc.sync.dma_start(
+                out=t[:].rearrange("p (j d) -> p j d", d=D), in_=tg_v[:, j0 : j0 + cnt, :]
+            )
+            for i in range(cnt):
+                src[(j0 + i, 0)] = (t[:].bitcast(F32), i * WORDS)
+
+        def load_neighbors():
+            j0, cnt = NB_CHUNKS[state["nb"]]
+            state["nb"] += 1
+            while state["tg"] < len(TG_CHUNKS) and TG_CHUNKS[state["tg"]][0] <= j0:
+                load_targets()
+            t = nbp.tile([P, cnt * NBRS * D], BF16, name="nb")
+            nc.sync.dma_start(
+                out=t[:].rearrange("p (j f) -> p j f", f=NBRS * D), in_=nb_v[:, j0 : j0 + cnt, :]
+            )
+            for i in range(cnt):
+                for n in range(NBRS):
+                    src[(j0 + i, n + 1)] = (t[:].bitcast(F32), (i * NBRS + n) * WORDS)
+
+        load_neighbors()
+
+        w_raw = const.tile([P, 4 * L], BF16, name="w_raw")
+        nc.sync.dma_start(out=w_raw[:], in_=w_v)
+        a_sb = const.tile([P, TILES * MEMBERS], BF16, name="a_sb")
+        nc.sync.dma_start(out=a_sb[:], in_=a_v)
+
+        for c in range(1, NB_BUFS):
+            load_neighbors()
+
+        w_grp = const.tile([P, L * 4], BF16, name="w_grp", align_bytes=64)
+        nc.vector.tensor_copy(
+            out=w_grp[:].rearrange("q (c t) -> q c t", t=4),
+            in_=w_raw[:].rearrange("q (t c) -> q c t", t=4),
+        )
+        w_codes = const.tile([P, L], U32, name="w_codes", align_bytes=64)
+        w_scales = const.tile([P, L], U8, name="w_scales", align_bytes=64)
+
+        deg = const.tile([P, TILES], F32, name="deg")
+        nc.vector.tensor_reduce(
+            out=deg[:],
+            in_=a_sb[:].rearrange("p (j k) -> p j k", k=MEMBERS),
+            axis=mybir.AxisListType.X,
+            op=ALU.add,
+        )
+        nc.vector.quantize_mx(out=w_codes[:].bitcast(FP8X4), scales=w_scales[:], in_=w_grp[:])
+        big = const.tile([P, TILES], F32, name="big")
+        nc.vector.tensor_single_scalar(out=big[:], in_=deg[:], scalar=0.5, op=ALU.is_gt)
+        kept = const.tile([P, TILES], F32, name="kept")
+        nc.vector.tensor_tensor(out=kept[:], in0=deg[:], in1=big[:], op=ALU.mult)
+        small = const.tile([P, TILES], F32, name="small")
+        nc.vector.tensor_scalar(
+            out=small[:], in0=big[:], scalar1=-1.0, scalar2=1.0, op0=ALU.mult, op1=ALU.add
+        )
+        factor = const.tile([P, TILES], F32, name="factor")
+        nc.vector.tensor_tensor(out=factor[:], in0=kept[:], in1=small[:], op=ALU.add)
+        recip = const.tile([P, TILES], F32, name="recip")
+        nc.vector.reciprocal(out=recip[:], in_=factor[:])
+
+        quantised = {}
+        stores = {}
+
+        def transpose_and_quantise(j):
+            g = grp.tile([P, MEMBERS * P * 4], BF16, name="g", align_bytes=64)
+            g32 = g[:].bitcast(F32)
+            for b in range(MEMBERS // 2):
+                xt = pst.tile([P, 4 * P], F32, name="xt")
+                for mm in range(2):
+                    view, w0 = src[(j, 2 * b + mm)]
+                    for u in range(2):
+                        nc.tensor.transpose(
+                            xt[:, (2 * mm + u) * P : (2 * mm + u + 1) * P],
+                            view[:, w0 + u : w0 + WORDS : 2],
+                            ident[:],
+                        )
+                dst = g32[:, b * 4 * P : (b + 1) * 4 * P].rearrange("p (m r u) -> p m r u", m=2, u=2)
+                bank = xt[:].rearrange("p (m u r) -> p m r u", m=2, u=2)
+                if b in VECTOR_BANKS[j % 2]:
+                    nc.vector.tensor_copy(out=dst, in_=bank)
+                else:
+                    nc.scalar.copy(out=dst, in_=bank)
+            codes = qp.tile([P, MEMBERS * P], U32, name="codes", align_bytes=64)
+            scales = qp.tile([P, MEMBERS * P], U8, name="scales", align_bytes=64)
+            half = MEMBERS * P // 2
+            for h in range(2):
+                nc.vector.quantize_mx(
+                    out=codes[:, h * half : (h + 1) * half].bitcast(FP8X4),
+                    scales=scales[:, h * half : (h + 1) * half],
+                    in_=g[:, h * half * 4 : (h + 1) * half * 4],
+                )
+            quantised[j] = (codes, scales)
+
+        def multiply_and_store(j):
+            codes, scales = quantised[j]
+            acc = psa.tile([P, L], F32, name="acc")
+            for m in range(MEMBERS):
+                nc.tensor.matmul_mx(
+                    out=acc[:],
+                    lhsT=codes[:, m * P : (m + 1) * P].bitcast(FP8X4),
+                    lhsT_scale=scales[:, m * P : (m + 1) * P],
+                    rhs=w_codes[:].bitcast(FP8X4),
+                    rhs_scale=w_scales[:],
+                    start=(m == 0),
+                    stop=(m == MEMBERS - 1),
+                )
+            for j0, cnt in ST_CHUNKS:
+                if j0 <= j < j0 + cnt:
+                    if j == j0:
+                        stores[j0] = stp.tile([P, cnt * L], F32, name="res")
+                    res = stores[j0]
+                    nc.scalar.activation(
+                        out=res[:, (j - j0) * L : (j - j0 + 1) * L],
+                        in_=acc[:],
+                        func=ACT.Relu,
+                        scale=recip[:, j : j + 1],
+                    )
+                    if j == j0 + cnt - 1:
+                        nc.scalar.dma_start(
+                            out=out_v[:, j0 : j0 + cnt, :],
+                            in_=res[:].rearrange("p (j l) -> p j l", l=L),
+                        )
+
+        starts = [sum(RUNS[:s]) for s in range(len(RUNS))]
+        for s in range(len(RUNS) + 1):
+            if s < len(RUNS):
+                for j in range(starts[s], starts[s] + RUNS[s]):
+                    transpose_and_quantise(j)
+                    while state["nb"] < len(NB_CHUNKS):
+                        j0, cnt = NB_CHUNKS[state["nb"] - NB_BUFS]
+                        if j0 + cnt - 1 > j:
+                            break
+                        load_neighbors()
+            if s >= 1:
+                for j in range(starts[s - 1], starts[s - 1] + RUNS[s - 1]):
+                    multiply_and_store(j)

@@ -22,12 +22,11 @@ WORDS = D // 2
 
 FLOPS = 2 * NODES * MEMBERS * D * L
 
-RUNS = [1] * 32
-NB_CHUNKS = [(0, 1), (1, 1)] + [(j, 2) for j in range(2, 30, 2)] + [(30, 1), (31, 1)]
-TG_CHUNKS = [(0, 1), (1, 3), (4, 4), (8, 8), (16, 8), (24, 8)]
+NB_CHUNKS = [(j, 1) for j in range(32)]
+TG_CHUNKS = [(0, 1), (1, 3)] + [(j, 4) for j in range(4, 32, 4)]
 ST_CHUNKS = [(j, 4) for j in range(0, 28, 4)] + [(28, 2), (30, 1), (31, 1)]
-NB_BUFS = 6
-VECTOR_BANKS = ((3,), (1, 3))
+NB_BUFS = 8
+VECTOR_BANKS = ((), (3,))
 
 
 def tile_singlegcnlayer_t_kernel(tc, targets, neighbors, a, kernel, out):
@@ -41,8 +40,11 @@ def tile_singlegcnlayer_t_kernel(tc, targets, neighbors, a, kernel, out):
     with ExitStack() as ctx:
         const = ctx.enter_context(tc.tile_pool(name="const", bufs=1))
         nbp = ctx.enter_context(tc.tile_pool(name="nbp", bufs=NB_BUFS))
-        grp = ctx.enter_context(tc.tile_pool(name="grp", bufs=4))
-        qp = ctx.enter_context(tc.tile_pool(name="qp", bufs=4))
+        tgp = ctx.enter_context(tc.tile_pool(name="tgp", bufs=4))
+        sbp = ctx.enter_context(tc.tile_pool(name="sbp", bufs=3))
+        stg = ctx.enter_context(tc.tile_pool(name="stg", bufs=2))
+        grp = ctx.enter_context(tc.tile_pool(name="grp", bufs=3))
+        qp = ctx.enter_context(tc.tile_pool(name="qp", bufs=3))
         stp = ctx.enter_context(tc.tile_pool(name="stp", bufs=3))
         pst = ctx.enter_context(tc.psum_pool(name="pst", bufs=6))
         psa = ctx.enter_context(tc.psum_pool(name="psa", bufs=2))
@@ -53,31 +55,27 @@ def tile_singlegcnlayer_t_kernel(tc, targets, neighbors, a, kernel, out):
         warm = const.tile([P, 1], F32, name="warm")
         nc.scalar.activation(out=warm[:], in_=ident[:, 0:1], func=ACT.Relu)
 
-        src = {}
+        raw_tg = {}
+        raw_nb = {}
         state = {"nb": 0, "tg": 0}
 
         def load_targets():
             j0, cnt = TG_CHUNKS[state["tg"]]
             state["tg"] += 1
-            t = const.tile([P, cnt * D], BF16, name="tg%d" % j0)
+            t = tgp.tile([P, cnt * D], BF16, name="tg")
             nc.sync.dma_start(
                 out=t[:].rearrange("p (j d) -> p j d", d=D), in_=tg_v[:, j0 : j0 + cnt, :]
             )
-            for i in range(cnt):
-                src[(j0 + i, 0)] = (t[:].bitcast(F32), i * WORDS)
+            raw_tg[j0] = t
 
         def load_neighbors():
             j0, cnt = NB_CHUNKS[state["nb"]]
             state["nb"] += 1
             while state["tg"] < len(TG_CHUNKS) and TG_CHUNKS[state["tg"]][0] <= j0:
                 load_targets()
-            t = nbp.tile([P, cnt * NBRS * D], BF16, name="nb")
-            nc.sync.dma_start(
-                out=t[:].rearrange("p (j f) -> p j f", f=NBRS * D), in_=nb_v[:, j0 : j0 + cnt, :]
-            )
-            for i in range(cnt):
-                for n in range(NBRS):
-                    src[(j0 + i, n + 1)] = (t[:].bitcast(F32), (i * NBRS + n) * WORDS)
+            t = nbp.tile([P, NBRS * D], BF16, name="nb")
+            nc.sync.dma_start(out=t[:], in_=nb_v[:, j0, :])
+            raw_nb[j0] = t
 
         load_neighbors()
 
@@ -88,6 +86,32 @@ def tile_singlegcnlayer_t_kernel(tc, targets, neighbors, a, kernel, out):
 
         for c in range(1, NB_BUFS):
             load_neighbors()
+
+        src = {}
+
+        def split_words(j):
+            for j0, cnt in TG_CHUNKS:
+                if j0 == j:
+                    n = cnt * P
+                    t = stg.tile([P, cnt * WORDS], F32, name="tg_split")
+                    nc.vector.tensor_copy(
+                        out=t[:].rearrange("p (u q) -> p u q", u=2),
+                        in_=raw_tg[j0][:].bitcast(F32).rearrange("p (q u) -> p u q", u=2),
+                    )
+                    for i in range(cnt):
+                        for u in range(2):
+                            src[(j0 + i, 0, u)] = (t, u * n + i * P)
+            n = NBRS * P
+            t = sbp.tile([P, NBRS * WORDS], F32, name="nb_split")
+            raw = raw_nb[j][:].bitcast(F32).rearrange("p (q u) -> p u q", u=2)
+            dst = t[:].rearrange("p (u q) -> p u q", u=2)
+            for lo, hi in ((0, 3), (3, 7)):
+                nc.vector.tensor_copy(out=dst[:, :, lo * P : hi * P], in_=raw[:, :, lo * P : hi * P])
+            for m in range(NBRS):
+                for u in range(2):
+                    src[(j, m + 1, u)] = (t, u * n + m * P)
+
+        split_words(0)
 
         w_grp = const.tile([P, L * 4], BF16, name="w_grp", align_bytes=64)
         nc.vector.tensor_copy(
@@ -127,11 +151,11 @@ def tile_singlegcnlayer_t_kernel(tc, targets, neighbors, a, kernel, out):
             for b in range(MEMBERS // 2):
                 xt = pst.tile([P, 4 * P], F32, name="xt")
                 for mm in range(2):
-                    view, w0 = src[(j, 2 * b + mm)]
                     for u in range(2):
+                        t, w0 = src[(j, 2 * b + mm, u)]
                         nc.tensor.transpose(
                             xt[:, (2 * mm + u) * P : (2 * mm + u + 1) * P],
-                            view[:, w0 + u : w0 + WORDS : 2],
+                            t[:, w0 : w0 + P],
                             ident[:],
                         )
                 dst = g32[:, b * 4 * P : (b + 1) * 4 * P].rearrange("p (m r u) -> p m r u", m=2, u=2)
@@ -181,16 +205,12 @@ def tile_singlegcnlayer_t_kernel(tc, targets, neighbors, a, kernel, out):
                             in_=res[:].rearrange("p (j l) -> p j l", l=L),
                         )
 
-        starts = [sum(RUNS[:s]) for s in range(len(RUNS))]
-        for s in range(len(RUNS) + 1):
-            if s < len(RUNS):
-                for j in range(starts[s], starts[s] + RUNS[s]):
-                    transpose_and_quantise(j)
-                    while state["nb"] < len(NB_CHUNKS):
-                        j0, cnt = NB_CHUNKS[state["nb"] - NB_BUFS]
-                        if j0 + cnt - 1 > j:
-                            break
+        for s in range(TILES + 1):
+            if s < TILES:
+                if s + 1 < TILES:
+                    split_words(s + 1)
+                    if state["nb"] < TILES:
                         load_neighbors()
+                transpose_and_quantise(s)
             if s >= 1:
-                for j in range(starts[s - 1], starts[s - 1] + RUNS[s - 1]):
-                    multiply_and_store(j)
+                multiply_and_store(s - 1)

@@ -26,7 +26,7 @@ NB_CHUNKS = [(j, 1) for j in range(32)]
 TG_CHUNKS = [(0, 1), (1, 3)] + [(j, 4) for j in range(4, 32, 4)]
 ST_CHUNKS = [(j, 4) for j in range(0, 28, 4)] + [(28, 2), (30, 1), (31, 1)]
 NB_BUFS = 8
-VECTOR_BANKS = ((), (3,))
+VECTOR_BANKS = ((), ())
 
 
 def tile_singlegcnlayer_t_kernel(tc, targets, neighbors, a, kernel, out):
@@ -200,7 +200,7 @@ def tile_singlegcnlayer_t_kernel(tc, targets, neighbors, a, kernel, out):
                         scale=recip[:, j : j + 1],
                     )
                     if j == j0 + cnt - 1:
-                        nc.scalar.dma_start(
+                        nc.sync.dma_start(
                             out=out_v[:, j0 : j0 + cnt, :],
                             in_=res[:].rearrange("p (j l) -> p j l", l=L),
                         )

@@ -27,6 +27,7 @@ TG_CHUNKS = [(0, 1), (1, 3)] + [(j, 4) for j in range(4, 32, 4)]
 ST_CHUNKS = [(j, 4) for j in range(0, 28, 4)] + [(28, 2), (30, 1), (31, 1)]
 NB_BUFS = 8
 VECTOR_BANKS = ((), ())
+RUNS = [1] + [2] * 15 + [1]
 
 
 def tile_singlegcnlayer_t_kernel(tc, targets, neighbors, a, kernel, out):
@@ -41,10 +42,10 @@ def tile_singlegcnlayer_t_kernel(tc, targets, neighbors, a, kernel, out):
         const = ctx.enter_context(tc.tile_pool(name="const", bufs=1))
         nbp = ctx.enter_context(tc.tile_pool(name="nbp", bufs=NB_BUFS))
         tgp = ctx.enter_context(tc.tile_pool(name="tgp", bufs=4))
-        sbp = ctx.enter_context(tc.tile_pool(name="sbp", bufs=3))
+        sbp = ctx.enter_context(tc.tile_pool(name="sbp", bufs=4))
         stg = ctx.enter_context(tc.tile_pool(name="stg", bufs=2))
-        grp = ctx.enter_context(tc.tile_pool(name="grp", bufs=3))
-        qp = ctx.enter_context(tc.tile_pool(name="qp", bufs=3))
+        grp = ctx.enter_context(tc.tile_pool(name="grp", bufs=4))
+        qp = ctx.enter_context(tc.tile_pool(name="qp", bufs=4))
         stp = ctx.enter_context(tc.tile_pool(name="stp", bufs=3))
         pst = ctx.enter_context(tc.psum_pool(name="pst", bufs=6))
         psa = ctx.enter_context(tc.psum_pool(name="psa", bufs=2))
@@ -205,12 +206,18 @@ def tile_singlegcnlayer_t_kernel(tc, targets, neighbors, a, kernel, out):
                             in_=res[:].rearrange("p (j l) -> p j l", l=L),
                         )
 
-        for s in range(TILES + 1):
-            if s < TILES:
-                if s + 1 < TILES:
-                    split_words(s + 1)
+        starts = [sum(RUNS[:s]) for s in range(len(RUNS))]
+        runs = [list(range(j0, j0 + cnt)) for j0, cnt in zip(starts, RUNS)]
+        for s in range(len(runs) + 1):
+            now = runs[s] if s < len(runs) else []
+            ahead = runs[s + 1] if s + 1 < len(runs) else []
+            for i in range(max(len(now), len(ahead))):
+                if i < len(ahead):
+                    split_words(ahead[i])
                     if state["nb"] < TILES:
                         load_neighbors()
-                transpose_and_quantise(s)
+                if i < len(now):
+                    transpose_and_quantise(now[i])
             if s >= 1:
-                multiply_and_store(s - 1)
+                for j in runs[s - 1]:
+                    multiply_and_store(j)

@@ -22,11 +22,11 @@ WORDS = D // 2
 
 FLOPS = 2 * NODES * MEMBERS * D * L
 
-NB_CHUNKS = [(j, 1) for j in range(32)]
-TG_CHUNKS = [(0, 1), (1, 3)] + [(j, 4) for j in range(4, 32, 4)]
+FIRST_PIECES = [(0, 2), (2, 5), (5, 8)]
+PIECES = [(0, 4), (4, 8)]
 ST_CHUNKS = [(j, 4) for j in range(0, 28, 4)] + [(28, 2), (30, 1), (31, 1)]
 NB_BUFS = 8
-VECTOR_BANKS = ((), ())
+VECTOR_BANKS = [(30, 3), (31, 1), (31, 3)]
 RUNS = [1] + [2] * 15 + [1]
 
 
@@ -41,9 +41,7 @@ def tile_singlegcnlayer_t_kernel(tc, targets, neighbors, a, kernel, out):
     with ExitStack() as ctx:
         const = ctx.enter_context(tc.tile_pool(name="const", bufs=1))
         nbp = ctx.enter_context(tc.tile_pool(name="nbp", bufs=NB_BUFS))
-        tgp = ctx.enter_context(tc.tile_pool(name="tgp", bufs=4))
         sbp = ctx.enter_context(tc.tile_pool(name="sbp", bufs=4))
-        stg = ctx.enter_context(tc.tile_pool(name="stg", bufs=2))
         grp = ctx.enter_context(tc.tile_pool(name="grp", bufs=4))
         qp = ctx.enter_context(tc.tile_pool(name="qp", bufs=4))
         stp = ctx.enter_context(tc.tile_pool(name="stp", bufs=3))
@@ -56,61 +54,44 @@ def tile_singlegcnlayer_t_kernel(tc, targets, neighbors, a, kernel, out):
         warm = const.tile([P, 1], F32, name="warm")
         nc.scalar.activation(out=warm[:], in_=ident[:, 0:1], func=ACT.Relu)
 
-        raw_tg = {}
-        raw_nb = {}
-        state = {"nb": 0, "tg": 0}
+        raw = {}
+        state = {"loaded": 0}
 
-        def load_targets():
-            j0, cnt = TG_CHUNKS[state["tg"]]
-            state["tg"] += 1
-            t = tgp.tile([P, cnt * D], BF16, name="tg")
-            nc.sync.dma_start(
-                out=t[:].rearrange("p (j d) -> p j d", d=D), in_=tg_v[:, j0 : j0 + cnt, :]
-            )
-            raw_tg[j0] = t
+        def load():
+            j = state["loaded"]
+            state["loaded"] += 1
+            t = nbp.tile([P, MEMBERS * D], BF16, name="x")
+            nc.sync.dma_start(out=t[:, 0:D], in_=tg_v[:, j, :])
+            for lo, hi in FIRST_PIECES if j == 0 else [(0, MEMBERS)]:
+                lo = max(lo, 1)
+                nc.sync.dma_start(
+                    out=t[:, lo * D : hi * D], in_=nb_v[:, j, (lo - 1) * D : (hi - 1) * D]
+                )
+            raw[j] = t
 
-        def load_neighbors():
-            j0, cnt = NB_CHUNKS[state["nb"]]
-            state["nb"] += 1
-            while state["tg"] < len(TG_CHUNKS) and TG_CHUNKS[state["tg"]][0] <= j0:
-                load_targets()
-            t = nbp.tile([P, NBRS * D], BF16, name="nb")
-            nc.sync.dma_start(out=t[:], in_=nb_v[:, j0, :])
-            raw_nb[j0] = t
-
-        load_neighbors()
+        load()
 
         w_raw = const.tile([P, 4 * L], BF16, name="w_raw")
         nc.sync.dma_start(out=w_raw[:], in_=w_v)
         a_sb = const.tile([P, TILES * MEMBERS], BF16, name="a_sb")
         nc.sync.dma_start(out=a_sb[:], in_=a_v)
 
-        for c in range(1, NB_BUFS):
-            load_neighbors()
+        for j in range(1, NB_BUFS):
+            load()
 
         src = {}
 
         def split_words(j):
-            for j0, cnt in TG_CHUNKS:
-                if j0 == j:
-                    n = cnt * P
-                    t = stg.tile([P, cnt * WORDS], F32, name="tg_split")
-                    nc.vector.tensor_copy(
-                        out=t[:].rearrange("p (u q) -> p u q", u=2),
-                        in_=raw_tg[j0][:].bitcast(F32).rearrange("p (q u) -> p u q", u=2),
-                    )
-                    for i in range(cnt):
-                        for u in range(2):
-                            src[(j0 + i, 0, u)] = (t, u * n + i * P)
-            n = NBRS * P
-            t = sbp.tile([P, NBRS * WORDS], F32, name="nb_split")
-            raw = raw_nb[j][:].bitcast(F32).rearrange("p (q u) -> p u q", u=2)
+            t = sbp.tile([P, MEMBERS * WORDS], F32, name="x_split")
             dst = t[:].rearrange("p (u q) -> p u q", u=2)
-            for lo, hi in ((0, 3), (3, 7)):
-                nc.vector.tensor_copy(out=dst[:, :, lo * P : hi * P], in_=raw[:, :, lo * P : hi * P])
-            for m in range(NBRS):
+            words = raw[j][:].bitcast(F32).rearrange("p (q u) -> p u q", u=2)
+            for lo, hi in FIRST_PIECES if j == 0 else PIECES:
+                nc.vector.tensor_copy(
+                    out=dst[:, :, lo * P : hi * P], in_=words[:, :, lo * P : hi * P]
+                )
+            for m in range(MEMBERS):
                 for u in range(2):
-                    src[(j, m + 1, u)] = (t, u * n + m * P)
+                    src[(j, m, u)] = t[:, (u * MEMBERS + m) * P : (u * MEMBERS + m + 1) * P]
 
         split_words(0)
 
@@ -130,16 +111,10 @@ def tile_singlegcnlayer_t_kernel(tc, targets, neighbors, a, kernel, out):
             op=ALU.add,
         )
         nc.vector.quantize_mx(out=w_codes[:].bitcast(FP8X4), scales=w_scales[:], in_=w_grp[:])
-        big = const.tile([P, TILES], F32, name="big")
-        nc.vector.tensor_single_scalar(out=big[:], in_=deg[:], scalar=0.5, op=ALU.is_gt)
-        kept = const.tile([P, TILES], F32, name="kept")
-        nc.vector.tensor_tensor(out=kept[:], in0=deg[:], in1=big[:], op=ALU.mult)
-        small = const.tile([P, TILES], F32, name="small")
-        nc.vector.tensor_scalar(
-            out=small[:], in0=big[:], scalar1=-1.0, scalar2=1.0, op0=ALU.mult, op1=ALU.add
-        )
         factor = const.tile([P, TILES], F32, name="factor")
-        nc.vector.tensor_tensor(out=factor[:], in0=kept[:], in1=small[:], op=ALU.add)
+        nc.vector.scalar_tensor_tensor(
+            out=factor[:], in0=deg[:], scalar=0.5, in1=deg[:], op0=ALU.is_le, op1=ALU.max
+        )
         recip = const.tile([P, TILES], F32, name="recip")
         nc.vector.reciprocal(out=recip[:], in_=factor[:])
 
@@ -153,22 +128,22 @@ def tile_singlegcnlayer_t_kernel(tc, targets, neighbors, a, kernel, out):
                 xt = pst.tile([P, 4 * P], F32, name="xt")
                 for mm in range(2):
                     for u in range(2):
-                        t, w0 = src[(j, 2 * b + mm, u)]
                         nc.tensor.transpose(
                             xt[:, (2 * mm + u) * P : (2 * mm + u + 1) * P],
-                            t[:, w0 : w0 + P],
+                            src[(j, 2 * b + mm, u)],
                             ident[:],
                         )
                 dst = g32[:, b * 4 * P : (b + 1) * 4 * P].rearrange("p (m r u) -> p m r u", m=2, u=2)
                 bank = xt[:].rearrange("p (m u r) -> p m r u", m=2, u=2)
-                if b in VECTOR_BANKS[j % 2]:
+                if (j, b) in VECTOR_BANKS:
                     nc.vector.tensor_copy(out=dst, in_=bank)
                 else:
                     nc.scalar.copy(out=dst, in_=bank)
             codes = qp.tile([P, MEMBERS * P], U32, name="codes", align_bytes=64)
             scales = qp.tile([P, MEMBERS * P], U8, name="scales", align_bytes=64)
-            half = MEMBERS * P // 2
-            for h in range(2):
+            parts = 4 if j == TILES - 1 else 2
+            half = MEMBERS * P // parts
+            for h in range(parts):
                 nc.vector.quantize_mx(
                     out=codes[:, h * half : (h + 1) * half].bitcast(FP8X4),
                     scales=scales[:, h * half : (h + 1) * half],
@@ -214,8 +189,8 @@ def tile_singlegcnlayer_t_kernel(tc, targets, neighbors, a, kernel, out):
             for i in range(max(len(now), len(ahead))):
                 if i < len(ahead):
                     split_words(ahead[i])
-                    if state["nb"] < TILES:
-                        load_neighbors()
+                    if state["loaded"] < TILES:
+                        load()
                 if i < len(now):
                     transpose_and_quantise(now[i])
             if s >= 1:

@@ -111,10 +111,16 @@ def tile_singlegcnlayer_t_kernel(tc, targets, neighbors, a, kernel, out):
             op=ALU.add,
         )
         nc.vector.quantize_mx(out=w_codes[:].bitcast(FP8X4), scales=w_scales[:], in_=w_grp[:])
-        factor = const.tile([P, TILES], F32, name="factor")
-        nc.vector.scalar_tensor_tensor(
-            out=factor[:], in0=deg[:], scalar=0.5, in1=deg[:], op0=ALU.is_le, op1=ALU.max
+        big = const.tile([P, TILES], F32, name="big")
+        nc.vector.tensor_single_scalar(out=big[:], in_=deg[:], scalar=0.5, op=ALU.is_gt)
+        kept = const.tile([P, TILES], F32, name="kept")
+        nc.vector.tensor_tensor(out=kept[:], in0=deg[:], in1=big[:], op=ALU.mult)
+        small = const.tile([P, TILES], F32, name="small")
+        nc.vector.tensor_scalar(
+            out=small[:], in0=big[:], scalar1=-1.0, scalar2=1.0, op0=ALU.mult, op1=ALU.add
         )
+        factor = const.tile([P, TILES], F32, name="factor")
+        nc.vector.tensor_tensor(out=factor[:], in0=kept[:], in1=small[:], op=ALU.add)
         recip = const.tile([P, TILES], F32, name="recip")
         nc.vector.reciprocal(out=recip[:], in_=factor[:])
 

from contextlib import ExitStack

import concourse.mybir as mybir
from concourse.masks import make_identity

F32 = mybir.dt.float32
BF16 = mybir.dt.bfloat16
U32 = mybir.dt.uint32
U8 = mybir.dt.uint8
FP8X4 = mybir.dt.float8_e4m3fn_x4
ALU = mybir.AluOpType
ACT = mybir.ActivationFunctionType

P = 128
NODES = 4096
TILES = NODES // P
NBRS = 7
MEMBERS = NBRS + 1
D = 512
L = 256
WORDS = D // 2

FLOPS = 2 * NODES * MEMBERS * D * L

FIRST_PIECES = [(0, 2), (2, 5), (5, 8)]
PIECES = [(0, 4), (4, 8)]
ST_CHUNKS = [(j, 4) for j in range(0, 28, 4)] + [(28, 2), (30, 1), (31, 1)]
NB_BUFS = 8
VECTOR_BANKS = [(30, 3), (31, 1), (31, 3)]
RUNS = [1] + [2] * 15 + [1]


def tile_singlegcnlayer_t_kernel(tc, targets, neighbors, a, kernel, out):
    nc = tc.nc
    tg_v = targets.rearrange("b n d -> (b n) d").rearrange("(p j) d -> p j d", j=TILES)
    nb_v = neighbors.rearrange("b n k d -> (b n) (k d)").rearrange("(p j) f -> p j f", j=TILES)
    a_v = a.rearrange("b n k -> (b n) k").rearrange("(p j) k -> p (j k)", j=TILES)
    out_v = out.rearrange("b n l -> (b n) l").rearrange("(p j) l -> p j l", j=TILES)
    w_v = kernel.rearrange("(q t) c -> q (t c)", t=4)

    with ExitStack() as ctx:
        const = ctx.enter_context(tc.tile_pool(name="const", bufs=1))
        nbp = ctx.enter_context(tc.tile_pool(name="nbp", bufs=NB_BUFS))
        sbp = ctx.enter_context(tc.tile_pool(name="sbp", bufs=4))
        grp = ctx.enter_context(tc.tile_pool(name="grp", bufs=4))
        qp = ctx.enter_context(tc.tile_pool(name="qp", bufs=4))
        stp = ctx.enter_context(tc.tile_pool(name="stp", bufs=3))
        pst = ctx.enter_context(tc.psum_pool(name="pst", bufs=6))
        psa = ctx.enter_context(tc.psum_pool(name="psa", bufs=2))
        ctx.enter_context(tc.manual_schedule())

        ident = const.tile([P, P], F32, name="ident")
        make_identity(nc, ident[:])
        warm = const.tile([P, 1], F32, name="warm")
        nc.scalar.activation(out=warm[:], in_=ident[:, 0:1], func=ACT.Relu)

        raw = {}
        state = {"loaded": 0}

        def load():
            j = state["loaded"]
            state["loaded"] += 1
            t = nbp.tile([P, MEMBERS * D], BF16, name="x")
            nc.sync.dma_start(out=t[:, 0:D], in_=tg_v[:, j, :])
            for lo, hi in FIRST_PIECES if j == 0 else [(0, MEMBERS)]:
                lo = max(lo, 1)
                nc.sync.dma_start(
                    out=t[:, lo * D : hi * D], in_=nb_v[:, j, (lo - 1) * D : (hi - 1) * D]
                )
            raw[j] = t

        load()

        w_raw = const.tile([P, 4 * L], BF16, name="w_raw")
        nc.sync.dma_start(out=w_raw[:], in_=w_v)
        a_sb = const.tile([P, TILES * MEMBERS], BF16, name="a_sb")
        nc.sync.dma_start(out=a_sb[:], in_=a_v)

        for j in range(1, NB_BUFS):
            load()

        src = {}

        def split_words(j):
            t = sbp.tile([P, MEMBERS * WORDS], F32, name="x_split")
            dst = t[:].rearrange("p (u q) -> p u q", u=2)
            words = raw[j][:].bitcast(F32).rearrange("p (q u) -> p u q", u=2)
            for lo, hi in FIRST_PIECES if j == 0 else PIECES:
                nc.vector.tensor_copy(
                    out=dst[:, :, lo * P : hi * P], in_=words[:, :, lo * P : hi * P]
                )
            for m in range(MEMBERS):
                for u in range(2):
                    src[(j, m, u)] = t[:, (u * MEMBERS + m) * P : (u * MEMBERS + m + 1) * P]

        split_words(0)

        w_grp = const.tile([P, L * 4], BF16, name="w_grp", align_bytes=64)
        nc.vector.tensor_copy(
            out=w_grp[:].rearrange("q (c t) -> q c t", t=4),
            in_=w_raw[:].rearrange("q (t c) -> q c t", t=4),
        )
        w_codes = const.tile([P, L], U32, name="w_codes", align_bytes=64)
        w_scales = const.tile([P, L], U8, name="w_scales", align_bytes=64)

        deg = const.tile([P, TILES], F32, name="deg")
        nc.vector.tensor_reduce(
            out=deg[:],
            in_=a_sb[:].rearrange("p (j k) -> p j k", k=MEMBERS),
            axis=mybir.AxisListType.X,
            op=ALU.add,
        )
        nc.vector.quantize_mx(out=w_codes[:].bitcast(FP8X4), scales=w_scales[:], in_=w_grp[:])
        big = const.tile([P, TILES], F32, name="big")
        nc.vector.tensor_single_scalar(out=big[:], in_=deg[:], scalar=0.5, op=ALU.is_gt)
        kept = const.tile([P, TILES], F32, name="kept")
        nc.vector.tensor_tensor(out=kept[:], in0=deg[:], in1=big[:], op=ALU.mult)
        small = const.tile([P, TILES], F32, name="small")
        nc.vector.tensor_scalar(
            out=small[:], in0=big[:], scalar1=-1.0, scalar2=1.0, op0=ALU.mult, op1=ALU.add
        )
        factor = const.tile([P, TILES], F32, name="factor")
        nc.vector.tensor_tensor(out=factor[:], in0=kept[:], in1=small[:], op=ALU.add)
        recip = const.tile([P, TILES], F32, name="recip")
        nc.vector.reciprocal(out=recip[:], in_=factor[:])

        quantised = {}
        stores = {}

        def transpose_and_quantise(j):
            g = grp.tile([P, MEMBERS * P * 4], BF16, name="g", align_bytes=64)
            g32 = g[:].bitcast(F32)
            for b in range(MEMBERS // 2):
                xt = pst.tile([P, 4 * P], F32, name="xt")
                for mm in range(2):
                    for u in range(2):
                        nc.tensor.transpose(
                            xt[:, (2 * mm + u) * P : (2 * mm + u + 1) * P],
                            src[(j, 2 * b + mm, u)],
                            ident[:],
                        )
                dst = g32[:, b * 4 * P : (b + 1) * 4 * P].rearrange("p (m r u) -> p m r u", m=2, u=2)
                bank = xt[:].rearrange("p (m u r) -> p m r u", m=2, u=2)
                if (j, b) in VECTOR_BANKS:
                    nc.vector.tensor_copy(out=dst, in_=bank)
                else:
                    nc.scalar.copy(out=dst, in_=bank)
            codes = qp.tile([P, MEMBERS * P], U32, name="codes", align_bytes=64)
            scales = qp.tile([P, MEMBERS * P], U8, name="scales", align_bytes=64)
            parts = 4 if j == TILES - 1 else 2
            half = MEMBERS * P // parts
            for h in range(parts):
                nc.vector.quantize_mx(
                    out=codes[:, h * half : (h + 1) * half].bitcast(FP8X4),
                    scales=scales[:, h * half : (h + 1) * half],
                    in_=g[:, h * half * 4 : (h + 1) * half * 4],
                )
            quantised[j] = (codes, scales)

        def multiply_and_store(j):
            codes, scales = quantised[j]
            acc = psa.tile([P, L], F32, name="acc")
            for m in range(MEMBERS):
                nc.tensor.matmul_mx(
                    out=acc[:],
                    lhsT=codes[:, m * P : (m + 1) * P].bitcast(FP8X4),
                    lhsT_scale=scales[:, m * P : (m + 1) * P],
                    rhs=w_codes[:].bitcast(FP8X4),
                    rhs_scale=w_scales[:],
                    start=(m == 0),
                    stop=(m == MEMBERS - 1),
                )
            for j0, cnt in ST_CHUNKS:
                if j0 <= j < j0 + cnt:
                    if j == j0:
                        stores[j0] = stp.tile([P, cnt * L], F32, name="res")
                    res = stores[j0]
                    nc.scalar.activation(
                        out=res[:, (j - j0) * L : (j - j0 + 1) * L],
                        in_=acc[:],
                        func=ACT.Relu,
                        scale=recip[:, j : j + 1],
                    )
                    if j == j0 + cnt - 1:
                        nc.sync.dma_start(
                            out=out_v[:, j0 : j0 + cnt, :],
                            in_=res[:].rearrange("p (j l) -> p j l", l=L),
                        )

        starts = [sum(RUNS[:s]) for s in range(len(RUNS))]
        runs = [list(range(j0, j0 + cnt)) for j0, cnt in zip(starts, RUNS)]
        for s in range(len(runs) + 1):
            now = runs[s] if s < len(runs) else []
            ahead = runs[s + 1] if s + 1 < len(runs) else []
            for i in range(max(len(now), len(ahead))):
                if i < len(ahead):
                    split_words(ahead[i])
                    if state["loaded"] < TILES:
                        load()
                if i < len(now):
                    transpose_and_quantise(now[i])
            if s >= 1:
                for j in runs[s - 1]:
                    multiply_and_store(j)
